import numpy as np
import ml_dtypes


def mxq(x, axis, fmt="e4m3"):
    dtype, down = {"e4m3": (ml_dtypes.float8_e4m3fn, 7), "e5m2": (ml_dtypes.float8_e5m2, 14)}[fmt]
    v = np.moveaxis(np.asarray(x, np.float32).astype(ml_dtypes.bfloat16).astype(np.float64), axis, -1)
    blocks = v.reshape(v.shape[:-1] + (-1, 32))
    amax = np.abs(blocks).max(-1, keepdims=True)
    byte = np.maximum(np.where(amax > 0, np.frexp(amax)[1] - 1 + 127, 0) - down, 1)
    scale = np.exp2(byte - 127.0)
    codes = (blocks / scale).astype(np.float32).astype(dtype).astype(np.float64)
    return np.moveaxis((codes * scale).reshape(v.shape), -1, axis)


WIDE = False


def mx_kscale(k):
    if not WIDE:
        return np.ones(k)
    levels = np.array([10, -10, 5, -5, 0])
    a = np.random.permutation(np.resize(levels, k // 512 * 4)).reshape(k // 512, 4)
    idx = np.arange(k)
    return np.exp2(a[idx // 512, idx % 128 // 32])


BF16 = ml_dtypes.bfloat16


def bf(x):
    return np.asarray(x, np.float32).astype(BF16)


def f64(x):
    return np.asarray(x).astype(np.float64)


B, N, I, O = 256, 24, 512, 256
WS = 0.7 / np.sqrt(I)


def setup_inputs():
    s = mx_kscale(I)
    return {"x": bf((np.random.standard_normal((B, N, I)) * s).reshape(B, N * I)),
            "w_self": bf(np.random.standard_normal((N, O, I)) * WS / s),
            "w_parent": bf(np.random.standard_normal((N - 1, O, I)) * WS / s),
            "bias": bf(np.random.standard_normal(N * O) * 0.5)}


def reference(x, w_self, w_parent, bias):
    xq = mxq(f64(x).reshape(B, N, I).transpose(1, 0, 2), 2, "e4m3")
    y_self = xq @ mxq(f64(w_self).transpose(0, 2, 1), 1, "e4m3")
    y_par = xq[:-1] @ mxq(f64(w_parent).transpose(0, 2, 1), 1, "e4m3")
    y = np.concatenate([y_self[:1], y_self[1:] + y_par], 0)
    return y.transpose(1, 0, 2).reshape(B, N * O) + f64(bias)

@@ -1,0 +1,198 @@
+from contextlib import ExitStack
+
+import concourse.mybir as mybir
+from concourse.masks import make_identity
+
+F32 = mybir.dt.float32
+BF16 = mybir.dt.bfloat16
+U32 = mybir.dt.uint32
+U8 = mybir.dt.uint8
+I32 = mybir.dt.int32
+FP8X4 = mybir.dt.float8_e4m3fn_x4
+ADD = mybir.AluOpType.add
+
+P = 128
+BATCH = 256
+NODES = 24
+CIN = 512
+COUT = 256
+FLOPS = 2 * BATCH * COUT * CIN * (2 * NODES - 1)
+
+RAW_BUFS = 8
+GRP_BUFS = 3
+CODE_BUFS = 3
+TP_BUFS = 5
+ACC_BUFS = 3
+LAG1_STEPS = 5
+TAIL_STEPS = 2
+STORES = ((0, 4), (4, 4), (8, 4), (12, 4), (16, 4), (20, 2), (22, 2))
+VECTOR_UNITS = (("s", 23),)
+VECTOR_BANKS = {"x": (0, 1), "p": (), "s": ()}
+
+
+def unit_list():
+    units = []
+    for g in range(5):
+        units.extend([("x", 4 * g, 4), ("p", 4 * g, 4), ("s", 4 * g, 4)])
+    units.extend([("x", 20, 4), ("p", 20, 2), ("s", 20, 2), ("p", 22, 1), ("s", 22, 1), ("s", 23, 1)])
+    return units
+
+
+def tile_skeletonlinear_pa_kernel(tc, x, w_self, w_parent, bias, out):
+    nc = tc.nc
+    x_v = x.rearrange("(h p) c -> p h c", h=2)
+    out_v = out.rearrange("(h p) c -> p h c", h=2)
+    w_rows = {
+        "s": w_self.rearrange("n o i -> (n o) i"),
+        "p": w_parent.rearrange("n o i -> (n o) i"),
+    }
+    units = unit_list()
+    n_units = len(units)
+    raws = {}
+    grps = {}
+    loc = {}
+    out_tiles = {}
+
+    with ExitStack() as ctx:
+        const = ctx.enter_context(tc.tile_pool(name="const", bufs=1))
+        rawp = ctx.enter_context(tc.tile_pool(name="rawp", bufs=RAW_BUFS))
+        grpp = ctx.enter_context(tc.tile_pool(name="grpp", bufs=GRP_BUFS))
+        codep = ctx.enter_context(tc.tile_pool(name="codep", bufs=CODE_BUFS))
+        outp = ctx.enter_context(tc.tile_pool(name="outp", bufs=1))
+        tpp = ctx.enter_context(tc.psum_pool(name="tpp", bufs=TP_BUFS))
+        accp = ctx.enter_context(tc.psum_pool(name="accp", bufs=ACC_BUFS))
+        ctx.enter_context(tc.manual_schedule())
+
+        def load(i):
+            kind, n0, g = units[i]
+            raw = rawp.tile([P, g * 1024], BF16, tag="raw", name="raw%d" % i)
+            if kind == "x":
+                nc.sync.dma_start(
+                    out=raw[:].rearrange("p (h c) -> p h c", h=2),
+                    in_=x_v[:, :, n0 * CIN : (n0 + g) * CIN],
+                )
+            else:
+                rows = w_rows[kind][n0 * COUT : (n0 + g) * COUT, :]
+                nc.sync.dma_start(out=raw[:], in_=rows.rearrange("(p t) i -> p (t i)", t=2 * g))
+            raws[i] = raw
+
+        def flip(i):
+            kind, n0, g = units[i]
+            grp = grpp.tile([P, g * 1024], BF16, tag="grp", name="grp%d" % i, align_bytes=64)
+            grps[i] = grp
+            rf = raws[i][:].bitcast(F32)
+            gf = grp[:].bitcast(F32)
+            for s in range(g):
+                tp = tpp.tile([P, 4, P], F32, tag="tp", name="tp%d_%d" % (i, s))
+                for j in range(4):
+                    if kind == "x":
+                        col = (j // 2) * g * 256 + s * 256 + (j % 2) * 128
+                    else:
+                        col = (4 * s + j) * 128
+                    nc.tensor.transpose(tp[:, j, :], rf[:, col : col + 128], ident[:])
+                if kind == "x":
+                    dst = gf[:, s * 512 : (s + 1) * 512].rearrange("p (h b u) -> p h b u", h=2, u=2)
+                    src = tp[:].rearrange("p (h u) b -> p h b u", u=2)
+                else:
+                    dst = gf.rearrange("p (c s j) -> p s c j", s=g, j=4)[:, s]
+                    src = tp[:].rearrange("p j c -> p c j")
+                if s in VECTOR_BANKS[kind] or (kind, n0) in VECTOR_UNITS:
+                    nc.vector.tensor_copy(out=dst, in_=src)
+                else:
+                    nc.scalar.copy(out=dst, in_=src)
+
+        def quantise(i):
+            kind, n0, g = units[i]
+            codes = codep.tile([P, g * 256], U32, tag=kind + "c", name="codes%d" % i, align_bytes=64)
+            scales = codep.tile([P, g * 256], U8, tag=kind + "k", name="scales%d" % i, align_bytes=64)
+            nc.vector.quantize_mx(out=codes[:].bitcast(FP8X4), scales=scales[:], in_=grps[i][:])
+            for m in range(g):
+                loc[(kind, n0 + m)] = (codes, scales, m * 256)
+
+        def spread_bias(g):
+            bps = accp.tile([P, 1024], BF16, tag="acc", name="bps%d" % g)
+            bbc = bias_all[:, g * 1024 : (g + 1) * 1024]
+            for c in range(2):
+                nc.tensor.matmul(
+                    out=bps[:, c * 512 : (c + 1) * 512],
+                    lhsT=ones[:],
+                    rhs=bias0[:, g * 1024 + c * 512 : g * 1024 + (c + 1) * 512],
+                    start=True,
+                    stop=True,
+                )
+            nc.scalar.copy(out=bbc, in_=bps[:])
+
+        def mx_pass(acc_cols, x_node, h, w_key, start, stop):
+            xc, xk, x0 = loc[("x", x_node)]
+            wc, wk, w0 = loc[w_key]
+            nc.tensor.matmul_mx(
+                out=acc_cols,
+                lhsT=xc[:, x0 + h * P : x0 + (h + 1) * P].bitcast(FP8X4),
+                lhsT_scale=xk[:, x0 + h * P : x0 + (h + 1) * P],
+                rhs=wc[:, w0 : w0 + COUT].bitcast(FP8X4),
+                rhs_scale=wk[:, w0 : w0 + COUT],
+                start=start,
+                stop=stop,
+            )
+
+        def node_pair(n):
+            g = [q for q in range(len(STORES)) if STORES[q][0] <= n < STORES[q][0] + STORES[q][1]][0]
+            if g not in out_tiles:
+                out_tiles[g] = outp.tile([P, 2, STORES[g][1] * COUT], F32, tag="ost%d" % g, name="ost%d" % g)
+            c0 = (n - STORES[g][0]) * COUT
+            for h in range(2):
+                acc = accp.tile([P, 2 * COUT], F32, tag="acc", name="acc%d_%d" % (n, h))
+                for m in range(2):
+                    cols = acc[:, m * COUT : (m + 1) * COUT]
+                    if n + m > 0:
+                        mx_pass(cols, n + m - 1, h, ("p", n + m - 1), True, False)
+                    mx_pass(cols, n + m, h, ("s", n + m), n + m == 0, True)
+                nc.vector.tensor_tensor(
+                    out=out_tiles[g][:, h, c0 : c0 + 2 * COUT],
+                    in0=acc[:],
+                    in1=bias_all[:, n * COUT : (n + 2) * COUT],
+                    op=ADD,
+                )
+
+        def ready(n):
+            keys = [("x", n), ("s", n)]
+            if n > 0:
+                keys.extend([("x", n - 1), ("p", n - 1)])
+            return all([key in usable for key in keys])
+
+        ident = const.tile([P, P], F32, name="ident")
+        make_identity(nc, ident[:])
+        bias0 = const.tile([P, NODES * COUT], BF16, name="bias0")
+        nc.vector.memset(bias0[:].bitcast(I32), 0)
+        bias_all = const.tile([P, NODES * COUT], BF16, name="bias_all")
+        ones = const.tile([P, P], BF16, name="ones")
+        nc.vector.memset(ones[:], 1.0)
+
+        for i in range(min(RAW_BUFS, n_units)):
+            load(i)
+            if i == 0:
+                nc.sync.dma_start(out=bias0[0:1, :], in_=bias.rearrange("(o c) -> o c", o=1))
+
+        next_node = 0
+        usable = set()
+        for i in range(n_units + 2):
+            if i < n_units:
+                flip(i)
+                if i + RAW_BUFS < n_units:
+                    load(i + RAW_BUFS)
+            if 0 < i <= n_units:
+                quantise(i - 1)
+            if i < NODES // 4:
+                spread_bias(i)
+            if i < LAG1_STEPS or i >= n_units - TAIL_STEPS:
+                for key in loc:
+                    usable.add(key)
+            while next_node < NODES and ready(next_node) and ready(next_node + 1):
+                node_pair(next_node)
+                next_node += 2
+            for key in loc:
+                usable.add(key)
+
+        for g in range(len(STORES)):
+            n0, cnt = STORES[g]
+            nc.sync.dma_start(out=out_v[:, :, n0 * COUT : (n0 + cnt) * COUT], in_=out_tiles[g][:])

@@ -25,9 +25,11 @@ TP_BUFS = 5
 ACC_BUFS = 3
 LAG1_STEPS = 5
 TAIL_STEPS = 2
+HOLD_FROM = 16
+MAX_PAIRS = 1
 STORES = ((0, 4), (4, 4), (8, 4), (12, 4), (16, 4), (20, 2), (22, 2))
-VECTOR_UNITS = (("s", 23),)
-VECTOR_BANKS = {"x": (0, 1), "p": (), "s": ()}
+VECTOR_UNITS = ()
+VECTOR_BANKS = {"x": (0,), "p": (), "s": ()}
 
 
 def unit_list():
@@ -187,9 +189,17 @@ def tile_skeletonlinear_pa_kernel(tc, x, w_self, w_parent, bias, out):
             if i < LAG1_STEPS or i >= n_units - TAIL_STEPS:
                 for key in loc:
                     usable.add(key)
-            while next_node < NODES and ready(next_node) and ready(next_node + 1):
+            pairs_left = MAX_PAIRS if i < n_units - 1 else NODES
+            while (
+                pairs_left > 0
+                and next_node < NODES
+                and ready(next_node)
+                and ready(next_node + 1)
+                and not HOLD_FROM <= i < n_units - 1
+            ):
                 node_pair(next_node)
                 next_node += 2
+                pairs_left -= 1
             for key in loc:
                 usable.add(key)
 

@@ -25,8 +25,8 @@ TP_BUFS = 5
 ACC_BUFS = 3
 LAG1_STEPS = 5
 TAIL_STEPS = 2
-HOLD_FROM = 16
-MAX_PAIRS = 1
+HOLD_FROM = 99
+BACKLOG = 2
 STORES = ((0, 4), (4, 4), (8, 4), (12, 4), (16, 4), (20, 2), (22, 2))
 VECTOR_UNITS = ()
 VECTOR_BANKS = {"x": (0,), "p": (), "s": ()}
@@ -137,24 +137,23 @@ def tile_skeletonlinear_pa_kernel(tc, x, w_self, w_parent, bias, out):
                 stop=stop,
             )
 
-        def node_pair(n):
+        def node_pair(n, h):
             g = [q for q in range(len(STORES)) if STORES[q][0] <= n < STORES[q][0] + STORES[q][1]][0]
             if g not in out_tiles:
                 out_tiles[g] = outp.tile([P, 2, STORES[g][1] * COUT], F32, tag="ost%d" % g, name="ost%d" % g)
             c0 = (n - STORES[g][0]) * COUT
-            for h in range(2):
-                acc = accp.tile([P, 2 * COUT], F32, tag="acc", name="acc%d_%d" % (n, h))
-                for m in range(2):
-                    cols = acc[:, m * COUT : (m + 1) * COUT]
-                    if n + m > 0:
-                        mx_pass(cols, n + m - 1, h, ("p", n + m - 1), True, False)
-                    mx_pass(cols, n + m, h, ("s", n + m), n + m == 0, True)
-                nc.vector.tensor_tensor(
-                    out=out_tiles[g][:, h, c0 : c0 + 2 * COUT],
-                    in0=acc[:],
-                    in1=bias_all[:, n * COUT : (n + 2) * COUT],
-                    op=ADD,
-                )
+            acc = accp.tile([P, 2 * COUT], F32, tag="acc", name="acc%d_%d" % (n, h))
+            for m in range(2):
+                cols = acc[:, m * COUT : (m + 1) * COUT]
+                if n + m > 0:
+                    mx_pass(cols, n + m - 1, h, ("p", n + m - 1), True, False)
+                mx_pass(cols, n + m, h, ("s", n + m), n + m == 0, True)
+            nc.vector.tensor_tensor(
+                out=out_tiles[g][:, h, c0 : c0 + 2 * COUT],
+                in0=acc[:],
+                in1=bias_all[:, n * COUT : (n + 2) * COUT],
+                op=ADD,
+            )
 
         def ready(n):
             keys = [("x", n), ("s", n)]
@@ -176,6 +175,7 @@ def tile_skeletonlinear_pa_kernel(tc, x, w_self, w_parent, bias, out):
                 nc.sync.dma_start(out=bias0[0:1, :], in_=bias.rearrange("(o c) -> o c", o=1))
 
         next_node = 0
+        todo = []
         usable = set()
         for i in range(n_units + 2):
             if i < n_units:
@@ -189,17 +189,15 @@ def tile_skeletonlinear_pa_kernel(tc, x, w_self, w_parent, bias, out):
             if i < LAG1_STEPS or i >= n_units - TAIL_STEPS:
                 for key in loc:
                     usable.add(key)
-            pairs_left = MAX_PAIRS if i < n_units - 1 else NODES
-            while (
-                pairs_left > 0
-                and next_node < NODES
-                and ready(next_node)
-                and ready(next_node + 1)
-                and not HOLD_FROM <= i < n_units - 1
-            ):
-                node_pair(next_node)
+            while next_node < NODES and ready(next_node) and ready(next_node + 1):
+                todo.extend([(next_node, 0), (next_node, 1)])
                 next_node += 2
-                pairs_left -= 1
+            quota = len(todo) if i >= n_units - 1 else (2 if len(todo) > BACKLOG else 1)
+            if HOLD_FROM <= i < n_units - 1:
+                quota = 0
+            for item in todo[:quota]:
+                node_pair(item[0], item[1])
+            todo = todo[quota:]
             for key in loc:
                 usable.add(key)
 

@@ -21,29 +21,29 @@ FLOPS = 2 * BATCH * COUT * CIN * (2 * NODES - 1)
 RAW_BUFS = 8
 GRP_BUFS = 3
 CODE_BUFS = 3
+X_CODE_BUFS = 5
 TP_BUFS = 5
 ACC_BUFS = 3
 LAG1_STEPS = 5
 TAIL_STEPS = 2
-HOLD_FROM = 99
 BACKLOG = 2
-STORES = ((0, 4), (4, 4), (8, 4), (12, 4), (16, 4), (20, 2), (22, 2))
-VECTOR_UNITS = ()
+BOTH = 2
+STORES = ((0, 12), (12, 4), (16, 4), (20, 2), (22, 2))
 VECTOR_BANKS = {"x": (0,), "p": (), "s": ()}
 
 
 def unit_list():
     units = []
     for g in range(5):
-        units.extend([("x", 4 * g, 4), ("p", 4 * g, 4), ("s", 4 * g, 4)])
-    units.extend([("x", 20, 4), ("p", 20, 2), ("s", 20, 2), ("p", 22, 1), ("s", 22, 1), ("s", 23, 1)])
+        units.extend([("x", 4 * g, 4, BOTH), ("p", 4 * g, 4, 0), ("s", 4 * g, 4, 0)])
+    units.extend([("x", 20, 4, BOTH), ("p", 20, 2, 0), ("s", 20, 2, 0)])
+    units.extend([("p", 22, 1, 0), ("s", 22, 1, 0), ("s", 23, 1, 0)])
     return units
 
 
 def tile_skeletonlinear_pa_kernel(tc, x, w_self, w_parent, bias, out):
     nc = tc.nc
     x_v = x.rearrange("(h p) c -> p h c", h=2)
-    out_v = out.rearrange("(h p) c -> p h c", h=2)
     w_rows = {
         "s": w_self.rearrange("n o i -> (n o) i"),
         "p": w_parent.rearrange("n o i -> (n o) i"),
@@ -65,72 +65,87 @@ def tile_skeletonlinear_pa_kernel(tc, x, w_self, w_parent, bias, out):
         accp = ctx.enter_context(tc.psum_pool(name="accp", bufs=ACC_BUFS))
         ctx.enter_context(tc.manual_schedule())
 
+        def banks_of(i):
+            kind, n0, cnt, h = units[i]
+            return cnt // 2 if kind == "x" and h != BOTH else cnt
+
         def load(i):
-            kind, n0, g = units[i]
-            raw = rawp.tile([P, g * 1024], BF16, tag="raw", name="raw%d" % i)
-            if kind == "x":
+            kind, n0, cnt, h = units[i]
+            raw = rawp.tile([P, banks_of(i) * 1024], BF16, tag="raw", name="raw%d" % i)
+            if kind == "x" and h == BOTH:
                 nc.sync.dma_start(
                     out=raw[:].rearrange("p (h c) -> p h c", h=2),
-                    in_=x_v[:, :, n0 * CIN : (n0 + g) * CIN],
+                    in_=x_v[:, :, n0 * CIN : (n0 + cnt) * CIN],
                 )
+            elif kind == "x":
+                nc.sync.dma_start(out=raw[:], in_=x[h * P : (h + 1) * P, n0 * CIN : (n0 + cnt) * CIN])
             else:
-                rows = w_rows[kind][n0 * COUT : (n0 + g) * COUT, :]
-                nc.sync.dma_start(out=raw[:], in_=rows.rearrange("(p t) i -> p (t i)", t=2 * g))
+                rows = w_rows[kind][n0 * COUT : (n0 + cnt) * COUT, :]
+                nc.sync.dma_start(out=raw[:], in_=rows.rearrange("(p t) i -> p (t i)", t=2 * cnt))
             raws[i] = raw
 
         def flip(i):
-            kind, n0, g = units[i]
-            grp = grpp.tile([P, g * 1024], BF16, tag="grp", name="grp%d" % i, align_bytes=64)
+            kind, n0, cnt, h = units[i]
+            banks = banks_of(i)
+            grp = grpp.tile([P, banks * 1024], BF16, tag="grp", name="grp%d" % i, align_bytes=64)
             grps[i] = grp
             rf = raws[i][:].bitcast(F32)
             gf = grp[:].bitcast(F32)
-            for s in range(g):
+            for s in range(banks):
                 tp = tpp.tile([P, 4, P], F32, tag="tp", name="tp%d_%d" % (i, s))
                 for j in range(4):
-                    if kind == "x":
-                        col = (j // 2) * g * 256 + s * 256 + (j % 2) * 128
+                    if kind == "x" and h == BOTH:
+                        col = (j // 2) * cnt * 256 + s * 256 + (j % 2) * 128
                     else:
                         col = (4 * s + j) * 128
                     nc.tensor.transpose(tp[:, j, :], rf[:, col : col + 128], ident[:])
                 if kind == "x":
-                    dst = gf[:, s * 512 : (s + 1) * 512].rearrange("p (h b u) -> p h b u", h=2, u=2)
-                    src = tp[:].rearrange("p (h u) b -> p h b u", u=2)
+                    dst = gf[:, s * 512 : (s + 1) * 512].rearrange("p (a b u) -> p a b u", a=2, u=2)
+                    src = tp[:].rearrange("p (a u) b -> p a b u", u=2)
                 else:
-                    dst = gf.rearrange("p (c s j) -> p s c j", s=g, j=4)[:, s]
+                    dst = gf.rearrange("p (c s j) -> p s c j", s=banks, j=4)[:, s]
                     src = tp[:].rearrange("p j c -> p c j")
-                if s in VECTOR_BANKS[kind] or (kind, n0) in VECTOR_UNITS:
+                if s in VECTOR_BANKS[kind]:
                     nc.vector.tensor_copy(out=dst, in_=src)
                 else:
                     nc.scalar.copy(out=dst, in_=src)
 
         def quantise(i):
-            kind, n0, g = units[i]
-            codes = codep.tile([P, g * 256], U32, tag=kind + "c", name="codes%d" % i, align_bytes=64)
-            scales = codep.tile([P, g * 256], U8, tag=kind + "k", name="scales%d" % i, align_bytes=64)
+            kind, n0, cnt, h = units[i]
+            width = banks_of(i) * 256
+            bufs = X_CODE_BUFS if kind == "x" else CODE_BUFS
+            codes = codep.tile([P, width], U32, tag=kind + "c", name="codes%d" % i, align_bytes=64, bufs=bufs)
+            scales = codep.tile([P, width], U8, tag=kind + "k", name="scales%d" % i, align_bytes=64, bufs=bufs)
             nc.vector.quantize_mx(out=codes[:].bitcast(FP8X4), scales=scales[:], in_=grps[i][:])
-            for m in range(g):
-                loc[(kind, n0 + m)] = (codes, scales, m * 256)
+            for m in range(cnt):
+                if kind == "x" and h == BOTH:
+                    loc[(kind, n0 + m, 0)] = (codes, scales, m * 256)
+                    loc[(kind, n0 + m, 1)] = (codes, scales, m * 256 + P)
+                elif kind == "x":
+                    loc[(kind, n0 + m, h)] = (codes, scales, m * P)
+                else:
+                    loc[(kind, n0 + m)] = (codes, scales, m * COUT)
 
         def spread_bias(g):
             bps = accp.tile([P, 1024], BF16, tag="acc", name="bps%d" % g)
-            bbc = bias_all[:, g * 1024 : (g + 1) * 1024]
             for c in range(2):
+                k = 2 * g + c
                 nc.tensor.matmul(
                     out=bps[:, c * 512 : (c + 1) * 512],
-                    lhsT=ones[:],
-                    rhs=bias0[:, g * 1024 + c * 512 : g * 1024 + (c + 1) * 512],
+                    lhsT=ident_bf[:, k : k + 1].to_broadcast([P, P]),
+                    rhs=bias_rows[:],
                     start=True,
                     stop=True,
                 )
-            nc.scalar.copy(out=bbc, in_=bps[:])
+            nc.scalar.copy(out=bias_all[:, g * 1024 : (g + 1) * 1024], in_=bps[:])
 
         def mx_pass(acc_cols, x_node, h, w_key, start, stop):
-            xc, xk, x0 = loc[("x", x_node)]
+            xc, xk, x0 = loc[("x", x_node, h)]
             wc, wk, w0 = loc[w_key]
             nc.tensor.matmul_mx(
                 out=acc_cols,
-                lhsT=xc[:, x0 + h * P : x0 + (h + 1) * P].bitcast(FP8X4),
-                lhsT_scale=xk[:, x0 + h * P : x0 + (h + 1) * P],
+                lhsT=xc[:, x0 : x0 + P].bitcast(FP8X4),
+                lhsT_scale=xk[:, x0 : x0 + P],
                 rhs=wc[:, w0 : w0 + COUT].bitcast(FP8X4),
                 rhs_scale=wk[:, w0 : w0 + COUT],
                 start=start,
@@ -156,23 +171,25 @@ def tile_skeletonlinear_pa_kernel(tc, x, w_self, w_parent, bias, out):
             )
 
         def ready(n):
-            keys = [("x", n), ("s", n)]
+            keys = [("x", n, 0), ("x", n, 1), ("s", n)]
             if n > 0:
-                keys.extend([("x", n - 1), ("p", n - 1)])
+                keys.extend([("x", n - 1, 0), ("x", n - 1, 1), ("p", n - 1)])
             return all([key in usable for key in keys])
 
+        bias_rows = const.tile([P, 512], BF16, name="bias_rows")
+        nc.vector.memset(bias_rows[:].bitcast(I32), 0)
         ident = const.tile([P, P], F32, name="ident")
         make_identity(nc, ident[:])
-        bias0 = const.tile([P, NODES * COUT], BF16, name="bias0")
-        nc.vector.memset(bias0[:].bitcast(I32), 0)
+        ident_bf = const.tile([P, P], BF16, name="ident_bf")
+        make_identity(nc, ident_bf[:])
         bias_all = const.tile([P, NODES * COUT], BF16, name="bias_all")
-        ones = const.tile([P, P], BF16, name="ones")
-        nc.vector.memset(ones[:], 1.0)
 
         for i in range(min(RAW_BUFS, n_units)):
             load(i)
             if i == 0:
-                nc.sync.dma_start(out=bias0[0:1, :], in_=bias.rearrange("(o c) -> o c", o=1))
+                nc.sync.dma_start(
+                    out=bias_rows[0 : NODES * COUT // 512, :], in_=bias.rearrange("(k c) -> k c", c=512)
+                )
 
         next_node = 0
         todo = []
@@ -193,8 +210,6 @@ def tile_skeletonlinear_pa_kernel(tc, x, w_self, w_parent, bias, out):
                 todo.extend([(next_node, 0), (next_node, 1)])
                 next_node += 2
             quota = len(todo) if i >= n_units - 1 else (2 if len(todo) > BACKLOG else 1)
-            if HOLD_FROM <= i < n_units - 1:
-                quota = 0
             for item in todo[:quota]:
                 node_pair(item[0], item[1])
             todo = todo[quota:]
@@ -203,4 +218,7 @@ def tile_skeletonlinear_pa_kernel(tc, x, w_self, w_parent, bias, out):
 
         for g in range(len(STORES)):
             n0, cnt = STORES[g]
-            nc.sync.dma_start(out=out_v[:, :, n0 * COUT : (n0 + cnt) * COUT], in_=out_tiles[g][:])
+            for h in range(2):
+                nc.sync.dma_start(
+                    out=out[h * P : (h + 1) * P, n0 * COUT : (n0 + cnt) * COUT], in_=out_tiles[g][:, h, :]
+                )

@@ -24,7 +24,7 @@ CODE_BUFS = 3
 X_CODE_BUFS = 5
 TP_BUFS = 5
 ACC_BUFS = 3
-LAG1_STEPS = 5
+LAG1_STEPS = 3
 TAIL_STEPS = 2
 BACKLOG = 2
 BOTH = 2
@@ -34,10 +34,11 @@ VECTOR_BANKS = {"x": (0,), "p": (), "s": ()}
 
 def unit_list():
     units = []
-    for g in range(5):
+    units.extend([("s", 0, 2, 0), ("x", 0, 2, BOTH), ("p", 0, 2, 0), ("s", 2, 2, 0), ("x", 2, 2, BOTH), ("p", 2, 2, 0)])
+    for g in range(1, 5):
         units.extend([("x", 4 * g, 4, BOTH), ("p", 4 * g, 4, 0), ("s", 4 * g, 4, 0)])
-    units.extend([("x", 20, 4, BOTH), ("p", 20, 2, 0), ("s", 20, 2, 0)])
-    units.extend([("p", 22, 1, 0), ("s", 22, 1, 0), ("s", 23, 1, 0)])
+    units.extend([("x", 20, 4, BOTH), ("s", 20, 2, 0), ("p", 20, 2, 0)])
+    units.extend([("s", 22, 1, 0), ("p", 22, 1, 0), ("s", 23, 1, 0)])
     return units
 
 

from contextlib import ExitStack

import concourse.mybir as mybir
from concourse.masks import make_identity

F32 = mybir.dt.float32
BF16 = mybir.dt.bfloat16
U32 = mybir.dt.uint32
U8 = mybir.dt.uint8
I32 = mybir.dt.int32
FP8X4 = mybir.dt.float8_e4m3fn_x4
ADD = mybir.AluOpType.add

P = 128
BATCH = 256
NODES = 24
CIN = 512
COUT = 256
FLOPS = 2 * BATCH * COUT * CIN * (2 * NODES - 1)

RAW_BUFS = 8
GRP_BUFS = 3
CODE_BUFS = 3
X_CODE_BUFS = 5
TP_BUFS = 5
ACC_BUFS = 3
LAG1_STEPS = 3
TAIL_STEPS = 2
BACKLOG = 2
BOTH = 2
STORES = ((0, 12), (12, 4), (16, 4), (20, 2), (22, 2))
VECTOR_BANKS = {"x": (0,), "p": (), "s": ()}


def unit_list():
    units = []
    units.extend([("s", 0, 2, 0), ("x", 0, 2, BOTH), ("p", 0, 2, 0), ("s", 2, 2, 0), ("x", 2, 2, BOTH), ("p", 2, 2, 0)])
    for g in range(1, 5):
        units.extend([("x", 4 * g, 4, BOTH), ("p", 4 * g, 4, 0), ("s", 4 * g, 4, 0)])
    units.extend([("x", 20, 4, BOTH), ("s", 20, 2, 0), ("p", 20, 2, 0)])
    units.extend([("s", 22, 1, 0), ("p", 22, 1, 0), ("s", 23, 1, 0)])
    return units


def tile_skeletonlinear_pa_kernel(tc, x, w_self, w_parent, bias, out):
    nc = tc.nc
    x_v = x.rearrange("(h p) c -> p h c", h=2)
    w_rows = {
        "s": w_self.rearrange("n o i -> (n o) i"),
        "p": w_parent.rearrange("n o i -> (n o) i"),
    }
    units = unit_list()
    n_units = len(units)
    raws = {}
    grps = {}
    loc = {}
    out_tiles = {}

    with ExitStack() as ctx:
        const = ctx.enter_context(tc.tile_pool(name="const", bufs=1))
        rawp = ctx.enter_context(tc.tile_pool(name="rawp", bufs=RAW_BUFS))
        grpp = ctx.enter_context(tc.tile_pool(name="grpp", bufs=GRP_BUFS))
        codep = ctx.enter_context(tc.tile_pool(name="codep", bufs=CODE_BUFS))
        outp = ctx.enter_context(tc.tile_pool(name="outp", bufs=1))
        tpp = ctx.enter_context(tc.psum_pool(name="tpp", bufs=TP_BUFS))
        accp = ctx.enter_context(tc.psum_pool(name="accp", bufs=ACC_BUFS))
        ctx.enter_context(tc.manual_schedule())

        def banks_of(i):
            kind, n0, cnt, h = units[i]
            return cnt // 2 if kind == "x" and h != BOTH else cnt

        def load(i):
            kind, n0, cnt, h = units[i]
            raw = rawp.tile([P, banks_of(i) * 1024], BF16, tag="raw", name="raw%d" % i)
            if kind == "x" and h == BOTH:
                nc.sync.dma_start(
                    out=raw[:].rearrange("p (h c) -> p h c", h=2),
                    in_=x_v[:, :, n0 * CIN : (n0 + cnt) * CIN],
                )
            elif kind == "x":
                nc.sync.dma_start(out=raw[:], in_=x[h * P : (h + 1) * P, n0 * CIN : (n0 + cnt) * CIN])
            else:
                rows = w_rows[kind][n0 * COUT : (n0 + cnt) * COUT, :]
                nc.sync.dma_start(out=raw[:], in_=rows.rearrange("(p t) i -> p (t i)", t=2 * cnt))
            raws[i] = raw

        def flip(i):
            kind, n0, cnt, h = units[i]
            banks = banks_of(i)
            grp = grpp.tile([P, banks * 1024], BF16, tag="grp", name="grp%d" % i, align_bytes=64)
            grps[i] = grp
            rf = raws[i][:].bitcast(F32)
            gf = grp[:].bitcast(F32)
            for s in range(banks):
                tp = tpp.tile([P, 4, P], F32, tag="tp", name="tp%d_%d" % (i, s))
                for j in range(4):
                    if kind == "x" and h == BOTH:
                        col = (j // 2) * cnt * 256 + s * 256 + (j % 2) * 128
                    else:
                        col = (4 * s + j) * 128
                    nc.tensor.transpose(tp[:, j, :], rf[:, col : col + 128], ident[:])
                if kind == "x":
                    dst = gf[:, s * 512 : (s + 1) * 512].rearrange("p (a b u) -> p a b u", a=2, u=2)
                    src = tp[:].rearrange("p (a u) b -> p a b u", u=2)
                else:
                    dst = gf.rearrange("p (c s j) -> p s c j", s=banks, j=4)[:, s]
                    src = tp[:].rearrange("p j c -> p c j")
                if s in VECTOR_BANKS[kind]:
                    nc.vector.tensor_copy(out=dst, in_=src)
                else:
                    nc.scalar.copy(out=dst, in_=src)

        def quantise(i):
            kind, n0, cnt, h = units[i]
            width = banks_of(i) * 256
            bufs = X_CODE_BUFS if kind == "x" else CODE_BUFS
            codes = codep.tile([P, width], U32, tag=kind + "c", name="codes%d" % i, align_bytes=64, bufs=bufs)
            scales = codep.tile([P, width], U8, tag=kind + "k", name="scales%d" % i, align_bytes=64, bufs=bufs)
            nc.vector.quantize_mx(out=codes[:].bitcast(FP8X4), scales=scales[:], in_=grps[i][:])
            for m in range(cnt):
                if kind == "x" and h == BOTH:
                    loc[(kind, n0 + m, 0)] = (codes, scales, m * 256)
                    loc[(kind, n0 + m, 1)] = (codes, scales, m * 256 + P)
                elif kind == "x":
                    loc[(kind, n0 + m, h)] = (codes, scales, m * P)
                else:
                    loc[(kind, n0 + m)] = (codes, scales, m * COUT)

        def spread_bias(g):
            bps = accp.tile([P, 1024], BF16, tag="acc", name="bps%d" % g)
            for c in range(2):
                k = 2 * g + c
                nc.tensor.matmul(
                    out=bps[:, c * 512 : (c + 1) * 512],
                    lhsT=ident_bf[:, k : k + 1].to_broadcast([P, P]),
                    rhs=bias_rows[:],
                    start=True,
                    stop=True,
                )
            nc.scalar.copy(out=bias_all[:, g * 1024 : (g + 1) * 1024], in_=bps[:])

        def mx_pass(acc_cols, x_node, h, w_key, start, stop):
            xc, xk, x0 = loc[("x", x_node, h)]
            wc, wk, w0 = loc[w_key]
            nc.tensor.matmul_mx(
                out=acc_cols,
                lhsT=xc[:, x0 : x0 + P].bitcast(FP8X4),
                lhsT_scale=xk[:, x0 : x0 + P],
                rhs=wc[:, w0 : w0 + COUT].bitcast(FP8X4),
                rhs_scale=wk[:, w0 : w0 + COUT],
                start=start,
                stop=stop,
            )

        def node_pair(n, h):
            g = [q for q in range(len(STORES)) if STORES[q][0] <= n < STORES[q][0] + STORES[q][1]][0]
            if g not in out_tiles:
                out_tiles[g] = outp.tile([P, 2, STORES[g][1] * COUT], F32, tag="ost%d" % g, name="ost%d" % g)
            c0 = (n - STORES[g][0]) * COUT
            acc = accp.tile([P, 2 * COUT], F32, tag="acc", name="acc%d_%d" % (n, h))
            for m in range(2):
                cols = acc[:, m * COUT : (m + 1) * COUT]
                if n + m > 0:
                    mx_pass(cols, n + m - 1, h, ("p", n + m - 1), True, False)
                mx_pass(cols, n + m, h, ("s", n + m), n + m == 0, True)
            nc.vector.tensor_tensor(
                out=out_tiles[g][:, h, c0 : c0 + 2 * COUT],
                in0=acc[:],
                in1=bias_all[:, n * COUT : (n + 2) * COUT],
                op=ADD,
            )

        def ready(n):
            keys = [("x", n, 0), ("x", n, 1), ("s", n)]
            if n > 0:
                keys.extend([("x", n - 1, 0), ("x", n - 1, 1), ("p", n - 1)])
            return all([key in usable for key in keys])

        bias_rows = const.tile([P, 512], BF16, name="bias_rows")
        nc.vector.memset(bias_rows[:].bitcast(I32), 0)
        ident = const.tile([P, P], F32, name="ident")
        make_identity(nc, ident[:])
        ident_bf = const.tile([P, P], BF16, name="ident_bf")
        make_identity(nc, ident_bf[:])
        bias_all = const.tile([P, NODES * COUT], BF16, name="bias_all")

        for i in range(min(RAW_BUFS, n_units)):
            load(i)
            if i == 0:
                nc.sync.dma_start(
                    out=bias_rows[0 : NODES * COUT // 512, :], in_=bias.rearrange("(k c) -> k c", c=512)
                )

        next_node = 0
        todo = []
        usable = set()
        for i in range(n_units + 2):
            if i < n_units:
                flip(i)
                if i + RAW_BUFS < n_units:
                    load(i + RAW_BUFS)
            if 0 < i <= n_units:
                quantise(i - 1)
            if i < NODES // 4:
                spread_bias(i)
            if i < LAG1_STEPS or i >= n_units - TAIL_STEPS:
                for key in loc:
                    usable.add(key)
            while next_node < NODES and ready(next_node) and ready(next_node + 1):
                todo.extend([(next_node, 0), (next_node, 1)])
                next_node += 2
            quota = len(todo) if i >= n_units - 1 else (2 if len(todo) > BACKLOG else 1)
            for item in todo[:quota]:
                node_pair(item[0], item[1])
            todo = todo[quota:]
            for key in loc:
                usable.add(key)

        for g in range(len(STORES)):
            n0, cnt = STORES[g]
            for h in range(2):
                nc.sync.dma_start(
                    out=out[h * P : (h + 1) * P, n0 * COUT : (n0 + cnt) * COUT], in_=out_tiles[g][:, h, :]
                )
